import numpy as np
import ml_dtypes

BF16 = ml_dtypes.bfloat16


def bf(x):
    return np.asarray(x, np.float32).astype(BF16)


def f32(x):
    return np.asarray(x, np.float32)


def f64(x):
    return np.asarray(x).astype(np.float64)


def striped(idx):
    return np.tile(idx.reshape(-1, 16).T, (8, 1))


D, S, N, M = 128, 256, 128, 512


def setup_inputs():
    return {
        'pe': bf(np.random.standard_normal((D, S))),
        'hid': bf(np.random.standard_normal((D, N))),
        'w2': bf(np.random.standard_normal((D, D)) * np.sqrt(2.0 / D)),
        'b2': f32(0.1 * np.random.standard_normal((D, 1))),
        'wqkv': bf(np.random.standard_normal((D, M - D)) / np.sqrt(D)),
        'bqkv': f32(0.1 * np.random.standard_normal((M - D, 1))),
        'offs': striped(np.random.permutation(np.tile(np.arange(S), 2))[:N]),
    }


def reference(pe, hid, w2, b2, wqkv, bqkv, offs):
    idx = offs[:16].T.reshape(-1)
    xin = f64(w2).T @ np.maximum(f64(hid), 0.0) + f64(b2)
    x = xin + f64(pe)[:, idx]
    return np.concatenate([f64(wqkv).T @ x + f64(bqkv), x], axis=0)

@@ -1,0 +1,75 @@
+import concourse.mybir as mybir
+from concourse.masks import make_identity
+
+BF16, F32, U16 = mybir.dt.bfloat16, mybir.dt.float32, mybir.dt.uint16
+ADD = mybir.AluOpType.add
+IDENTITY = mybir.ActivationFunctionType.Identity
+
+P = 128
+AGENTS = 256
+TOKENS = 128
+QKV_BLOCKS = 3
+
+FLOPS = 2 * P * TOKENS * (P + QKV_BLOCKS * P)
+
+
+def tile_reltok_kernel(tc, pe, hid, w2, b2, wqkv, bqkv, offs, out):
+    nc = tc.nc
+    with (
+        tc.tile_pool(name="held", bufs=1) as held,
+        tc.psum_pool(name="banks", bufs=1) as banks,
+    ):
+        offsets = held.tile([P, TOKENS // 16], U16, name="offsets")
+        hid_sb = held.tile([P, TOKENS], BF16, name="hid_sb")
+        w2_sb = held.tile([P, P], BF16, name="w2_sb")
+        pe_sb = held.tile([P, AGENTS], BF16, name="pe_sb")
+        wqkv_sb = held.tile([P, QKV_BLOCKS * P], BF16, name="wqkv_sb")
+        b2_sb = held.tile([P, 1], F32, name="b2_sb")
+        bqkv_sb = held.tile([P, QKV_BLOCKS], F32, name="bqkv_sb")
+        nc.sync.dma_start(hid_sb[:], hid)
+        nc.scalar.dma_start(w2_sb[:], w2)
+        nc.sync.dma_start(wqkv_sb[:], wqkv)
+        nc.scalar.dma_start(pe_sb[:], pe)
+        nc.sync.dma_start(offsets[:], offs)
+        nc.scalar.dma_start(b2_sb[:], b2)
+        with nc.allow_non_contiguous_dma(reason="bias: one float32 to a partition for each block"):
+            nc.sync.dma_start(bqkv_sb[:], bqkv.rearrange("(c p) o -> p (c o)", p=P))
+
+        identity = held.tile([P, P], BF16, name="identity")
+        make_identity(nc, identity[:])
+
+        scratch = held.tile([P, 1], F32, name="scratch")
+        nc.vector.memset(scratch[:], 0.0)
+        warmed = held.tile([P, 1], F32, name="warmed")
+        nc.scalar.activation(warmed[:], scratch[:], IDENTITY)
+
+        relu_hid = held.tile([P, TOKENS], BF16, name="relu_hid")
+        nc.vector.tensor_scalar_max(relu_hid[:], hid_sb[:], 0.0)
+
+        looked_up = pe_sb[:].indirect(offsets[:])
+        qkv_banks = [banks.tile([P, TOKENS], F32, name=f"qkv_bank{c}") for c in range(QKV_BLOCKS)]
+        x_xin_bank = banks.tile([P, 2 * TOKENS], F32, name="x_xin_bank")
+        x_ps = x_xin_bank[:, 0:TOKENS]
+        xin_ps = x_xin_bank[:, TOKENS : 2 * TOKENS]
+        for c in range(QKV_BLOCKS):
+            nc.tensor.matmul(qkv_banks[c][:], wqkv_sb[:, c * P : (c + 1) * P], looked_up, start=True, stop=False)
+        nc.tensor.matmul(x_ps, identity[:], looked_up, start=True, stop=False)
+
+        nc.tensor.matmul(x_ps, w2_sb[:], relu_hid[:], start=False, stop=True)
+        nc.tensor.matmul(xin_ps, w2_sb[:], relu_hid[:], start=True, stop=True)
+
+        xin_bf = held.tile([P, TOKENS], BF16, name="xin_bf")
+        nc.vector.tensor_scalar(xin_bf[:], xin_ps, b2_sb[:, 0:1], None, ADD)
+        x_sb = held.tile([P, TOKENS], F32, name="x_sb")
+        nc.scalar.activation(x_sb[:], x_ps, IDENTITY, bias=b2_sb[:, 0:1])
+        nc.scalar.dma_start(out[QKV_BLOCKS * P : (QKV_BLOCKS + 1) * P, :], x_sb[:])
+
+        for c in range(QKV_BLOCKS):
+            nc.tensor.matmul(qkv_banks[c][:], wqkv_sb[:, c * P : (c + 1) * P], xin_bf[:], start=False, stop=True)
+            block_sb = held.tile([P, TOKENS], F32, name=f"block_sb{c}")
+            if c % 2 == 0:
+                nc.vector.tensor_scalar(block_sb[:], qkv_banks[c][:], bqkv_sb[:, c : c + 1], None, ADD)
+                nc.sync.dma_start(out[c * P : (c + 1) * P, :], block_sb[:])
+            else:
+                nc.scalar.activation(block_sb[:], qkv_banks[c][:], IDENTITY, bias=bqkv_sb[:, c : c + 1])
+                nc.scalar.dma_start(out[c * P : (c + 1) * P, :], block_sb[:])

@@ -46,20 +46,22 @@ def tile_reltok_kernel(tc, pe, hid, w2, b2, wqkv, bqkv, offs, out):
         relu_hid = held.tile([P, TOKENS], BF16, name="relu_hid")
         nc.vector.tensor_scalar_max(relu_hid[:], hid_sb[:], 0.0)
 
-        looked_up = pe_sb[:].indirect(offsets[:])
         qkv_banks = [banks.tile([P, TOKENS], F32, name=f"qkv_bank{c}") for c in range(QKV_BLOCKS)]
         x_xin_bank = banks.tile([P, 2 * TOKENS], F32, name="x_xin_bank")
         x_ps = x_xin_bank[:, 0:TOKENS]
         xin_ps = x_xin_bank[:, TOKENS : 2 * TOKENS]
+
+        nc.tensor.matmul(xin_ps, w2_sb[:], relu_hid[:], start=True, stop=True)
+
+        looked_up = pe_sb[:].indirect(offsets[:])
+        nc.tensor.matmul(x_ps, identity[:], looked_up, start=True, stop=False)
         for c in range(QKV_BLOCKS):
             nc.tensor.matmul(qkv_banks[c][:], wqkv_sb[:, c * P : (c + 1) * P], looked_up, start=True, stop=False)
-        nc.tensor.matmul(x_ps, identity[:], looked_up, start=True, stop=False)
-
-        nc.tensor.matmul(x_ps, w2_sb[:], relu_hid[:], start=False, stop=True)
-        nc.tensor.matmul(xin_ps, w2_sb[:], relu_hid[:], start=True, stop=True)
 
         xin_bf = held.tile([P, TOKENS], BF16, name="xin_bf")
         nc.vector.tensor_scalar(xin_bf[:], xin_ps, b2_sb[:, 0:1], None, ADD)
+
+        nc.tensor.matmul(x_ps, w2_sb[:], relu_hid[:], start=False, stop=True)
         x_sb = held.tile([P, TOKENS], F32, name="x_sb")
         nc.scalar.activation(x_sb[:], x_ps, IDENTITY, bias=b2_sb[:, 0:1])
         nc.scalar.dma_start(out[QKV_BLOCKS * P : (QKV_BLOCKS + 1) * P, :], x_sb[:])

@@ -28,10 +28,10 @@ def tile_reltok_kernel(tc, pe, hid, w2, b2, wqkv, bqkv, offs, out):
         bqkv_sb = held.tile([P, QKV_BLOCKS], F32, name="bqkv_sb")
         nc.sync.dma_start(hid_sb[:], hid)
         nc.scalar.dma_start(w2_sb[:], w2)
+        nc.scalar.dma_start(b2_sb[:], b2)
         nc.sync.dma_start(wqkv_sb[:], wqkv)
         nc.scalar.dma_start(pe_sb[:], pe)
         nc.sync.dma_start(offsets[:], offs)
-        nc.scalar.dma_start(b2_sb[:], b2)
         with nc.allow_non_contiguous_dma(reason="bias: one float32 to a partition for each block"):
             nc.sync.dma_start(bqkv_sb[:], bqkv.rearrange("(c p) o -> p (c o)", p=P))
 
@@ -46,32 +46,26 @@ def tile_reltok_kernel(tc, pe, hid, w2, b2, wqkv, bqkv, offs, out):
         relu_hid = held.tile([P, TOKENS], BF16, name="relu_hid")
         nc.vector.tensor_scalar_max(relu_hid[:], hid_sb[:], 0.0)
 
-        qkv_banks = [banks.tile([P, TOKENS], F32, name=f"qkv_bank{c}") for c in range(QKV_BLOCKS)]
-        x_xin_bank = banks.tile([P, 2 * TOKENS], F32, name="x_xin_bank")
-        x_ps = x_xin_bank[:, 0:TOKENS]
-        xin_ps = x_xin_bank[:, TOKENS : 2 * TOKENS]
+        xin_bank = banks.tile([P, TOKENS], F32, name="xin_bank")
+        out_banks = [banks.tile([P, TOKENS], F32, name=f"out_bank{c}") for c in range(QKV_BLOCKS + 1)]
 
-        nc.tensor.matmul(xin_ps, w2_sb[:], relu_hid[:], start=True, stop=True)
+        nc.tensor.matmul(xin_bank[:], w2_sb[:], relu_hid[:], start=True, stop=True)
+        nc.tensor.matmul(out_banks[QKV_BLOCKS][:], w2_sb[:], relu_hid[:], start=True, stop=False)
+        xin_bf = held.tile([P, TOKENS], BF16, name="xin_bf")
+        nc.vector.tensor_scalar(xin_bf[:], xin_bank[:], b2_sb[:, 0:1], None, ADD)
+
+        for c in range(QKV_BLOCKS):
+            nc.tensor.matmul(out_banks[c][:], wqkv_sb[:, c * P : (c + 1) * P], xin_bf[:], start=True, stop=False)
 
         looked_up = pe_sb[:].indirect(offsets[:])
-        nc.tensor.matmul(x_ps, identity[:], looked_up, start=True, stop=False)
-        for c in range(QKV_BLOCKS):
-            nc.tensor.matmul(qkv_banks[c][:], wqkv_sb[:, c * P : (c + 1) * P], looked_up, start=True, stop=False)
-
-        xin_bf = held.tile([P, TOKENS], BF16, name="xin_bf")
-        nc.vector.tensor_scalar(xin_bf[:], xin_ps, b2_sb[:, 0:1], None, ADD)
-
-        nc.tensor.matmul(x_ps, w2_sb[:], relu_hid[:], start=False, stop=True)
-        x_sb = held.tile([P, TOKENS], F32, name="x_sb")
-        nc.scalar.activation(x_sb[:], x_ps, IDENTITY, bias=b2_sb[:, 0:1])
-        nc.scalar.dma_start(out[QKV_BLOCKS * P : (QKV_BLOCKS + 1) * P, :], x_sb[:])
-
-        for c in range(QKV_BLOCKS):
-            nc.tensor.matmul(qkv_banks[c][:], wqkv_sb[:, c * P : (c + 1) * P], xin_bf[:], start=False, stop=True)
+        for c in range(QKV_BLOCKS + 1):
+            weights = wqkv_sb[:, c * P : (c + 1) * P] if c < QKV_BLOCKS else identity[:]
+            bias = bqkv_sb[:, c : c + 1] if c < QKV_BLOCKS else b2_sb[:, 0:1]
+            nc.tensor.matmul(out_banks[c][:], weights, looked_up, start=False, stop=True)
             block_sb = held.tile([P, TOKENS], F32, name=f"block_sb{c}")
             if c % 2 == 0:
-                nc.vector.tensor_scalar(block_sb[:], qkv_banks[c][:], bqkv_sb[:, c : c + 1], None, ADD)
+                nc.vector.tensor_scalar(block_sb[:], out_banks[c][:], bias, None, ADD)
                 nc.sync.dma_start(out[c * P : (c + 1) * P, :], block_sb[:])
             else:
-                nc.scalar.activation(block_sb[:], qkv_banks[c][:], IDENTITY, bias=bqkv_sb[:, c : c + 1])
+                nc.scalar.activation(block_sb[:], out_banks[c][:], IDENTITY, bias=bias)
                 nc.scalar.dma_start(out[c * P : (c + 1) * P, :], block_sb[:])

@@ -10,6 +10,9 @@ AGENTS = 256
 TOKENS = 128
 QKV_BLOCKS = 3
 
+WARM_COLUMNS = 512
+WARM_MATMULS = 4
+
 FLOPS = 2 * P * TOKENS * (P + QKV_BLOCKS * P)
 
 
@@ -19,6 +22,12 @@ def tile_reltok_kernel(tc, pe, hid, w2, b2, wqkv, bqkv, offs, out):
         tc.tile_pool(name="held", bufs=1) as held,
         tc.psum_pool(name="banks", bufs=1) as banks,
     ):
+        zeros = held.tile([P, WARM_COLUMNS], BF16, name="zeros")
+        nc.vector.memset(zeros[:], 0.0)
+        warm_bank = banks.tile([P, WARM_COLUMNS], F32, name="warm_bank")
+        for w in range(WARM_MATMULS):
+            nc.tensor.matmul(warm_bank[:], zeros[:, 0:P], zeros[:], start=True, stop=True)
+
         offsets = held.tile([P, TOKENS // 16], U16, name="offsets")
         hid_sb = held.tile([P, TOKENS], BF16, name="hid_sb")
         w2_sb = held.tile([P, P], BF16, name="w2_sb")

@@ -1,17 +1,13 @@
 import concourse.mybir as mybir
-from concourse.masks import make_identity
 
 BF16, F32, U16 = mybir.dt.bfloat16, mybir.dt.float32, mybir.dt.uint16
-ADD = mybir.AluOpType.add
+ADD, MULT, IS_EQUAL = mybir.AluOpType.add, mybir.AluOpType.mult, mybir.AluOpType.is_equal
 IDENTITY = mybir.ActivationFunctionType.Identity
 
 P = 128
 AGENTS = 256
 TOKENS = 128
 QKV_BLOCKS = 3
-
-WARM_COLUMNS = 512
-WARM_MATMULS = 4
 
 FLOPS = 2 * P * TOKENS * (P + QKV_BLOCKS * P)
 
@@ -22,12 +18,6 @@ def tile_reltok_kernel(tc, pe, hid, w2, b2, wqkv, bqkv, offs, out):
         tc.tile_pool(name="held", bufs=1) as held,
         tc.psum_pool(name="banks", bufs=1) as banks,
     ):
-        zeros = held.tile([P, WARM_COLUMNS], BF16, name="zeros")
-        nc.vector.memset(zeros[:], 0.0)
-        warm_bank = banks.tile([P, WARM_COLUMNS], F32, name="warm_bank")
-        for w in range(WARM_MATMULS):
-            nc.tensor.matmul(warm_bank[:], zeros[:, 0:P], zeros[:], start=True, stop=True)
-
         offsets = held.tile([P, TOKENS // 16], U16, name="offsets")
         hid_sb = held.tile([P, TOKENS], BF16, name="hid_sb")
         w2_sb = held.tile([P, P], BF16, name="w2_sb")
@@ -44,37 +34,45 @@ def tile_reltok_kernel(tc, pe, hid, w2, b2, wqkv, bqkv, offs, out):
         with nc.allow_non_contiguous_dma(reason="bias: one float32 to a partition for each block"):
             nc.sync.dma_start(bqkv_sb[:], bqkv.rearrange("(c p) o -> p (c o)", p=P))
 
+        ones = held.tile([P, P], F32, name="ones")
+        nc.vector.memset(ones[:], 1.0)
+        column_index = held.tile([P, P], F32, name="column_index")
+        nc.vector.tensor_tensor_scan(column_index[:], ones[:], ones[:], -1.0, MULT, ADD)
+        row_index = banks.tile([P, 1], F32, name="row_index")
+        nc.tensor.matmul(row_index[:], column_index[0:1, :], ones[0:1, 0:1], start=True, stop=True)
         identity = held.tile([P, P], BF16, name="identity")
-        make_identity(nc, identity[:])
+        nc.vector.tensor_scalar(identity[:], column_index[:], row_index[:, 0:1], None, IS_EQUAL)
 
-        scratch = held.tile([P, 1], F32, name="scratch")
-        nc.vector.memset(scratch[:], 0.0)
         warmed = held.tile([P, 1], F32, name="warmed")
-        nc.scalar.activation(warmed[:], scratch[:], IDENTITY)
+        nc.scalar.activation(warmed[:], ones[:, 0:1], IDENTITY)
 
         relu_hid = held.tile([P, TOKENS], BF16, name="relu_hid")
         nc.vector.tensor_scalar_max(relu_hid[:], hid_sb[:], 0.0)
 
         xin_bank = banks.tile([P, TOKENS], F32, name="xin_bank")
-        out_banks = [banks.tile([P, TOKENS], F32, name=f"out_bank{c}") for c in range(QKV_BLOCKS + 1)]
+        x_bank = banks.tile([P, TOKENS], F32, name="x_bank")
+        qkv_banks = [banks.tile([P, TOKENS], F32, name=f"qkv_bank{c}") for c in range(QKV_BLOCKS)]
 
         nc.tensor.matmul(xin_bank[:], w2_sb[:], relu_hid[:], start=True, stop=True)
-        nc.tensor.matmul(out_banks[QKV_BLOCKS][:], w2_sb[:], relu_hid[:], start=True, stop=False)
+        nc.tensor.matmul(x_bank[:], w2_sb[:], relu_hid[:], start=True, stop=False)
         xin_bf = held.tile([P, TOKENS], BF16, name="xin_bf")
         nc.vector.tensor_scalar(xin_bf[:], xin_bank[:], b2_sb[:, 0:1], None, ADD)
 
-        for c in range(QKV_BLOCKS):
-            nc.tensor.matmul(out_banks[c][:], wqkv_sb[:, c * P : (c + 1) * P], xin_bf[:], start=True, stop=False)
-
         looked_up = pe_sb[:].indirect(offsets[:])
-        for c in range(QKV_BLOCKS + 1):
-            weights = wqkv_sb[:, c * P : (c + 1) * P] if c < QKV_BLOCKS else identity[:]
-            bias = bqkv_sb[:, c : c + 1] if c < QKV_BLOCKS else b2_sb[:, 0:1]
-            nc.tensor.matmul(out_banks[c][:], weights, looked_up, start=False, stop=True)
+        nc.tensor.matmul(x_bank[:], identity[:], looked_up, start=False, stop=True)
+        for c in range(QKV_BLOCKS):
+            nc.tensor.matmul(qkv_banks[c][:], wqkv_sb[:, c * P : (c + 1) * P], looked_up, start=True, stop=False)
+
+        x_sb = held.tile([P, TOKENS], F32, name="x_sb")
+        nc.scalar.activation(x_sb[:], x_bank[:], IDENTITY, bias=b2_sb[:, 0:1])
+        nc.scalar.dma_start(out[QKV_BLOCKS * P : (QKV_BLOCKS + 1) * P, :], x_sb[:])
+
+        for c in range(QKV_BLOCKS):
+            nc.tensor.matmul(qkv_banks[c][:], wqkv_sb[:, c * P : (c + 1) * P], xin_bf[:], start=False, stop=True)
             block_sb = held.tile([P, TOKENS], F32, name=f"block_sb{c}")
             if c % 2 == 0:
-                nc.vector.tensor_scalar(block_sb[:], out_banks[c][:], bias, None, ADD)
+                nc.vector.tensor_scalar(block_sb[:], qkv_banks[c][:], bqkv_sb[:, c : c + 1], None, ADD)
                 nc.sync.dma_start(out[c * P : (c + 1) * P, :], block_sb[:])
             else:
-                nc.scalar.activation(block_sb[:], out_banks[c][:], IDENTITY, bias=bias)
+                nc.scalar.activation(block_sb[:], qkv_banks[c][:], IDENTITY, bias=bqkv_sb[:, c : c + 1])
                 nc.scalar.dma_start(out[c * P : (c + 1) * P, :], block_sb[:])

@@ -23,16 +23,16 @@ def tile_reltok_kernel(tc, pe, hid, w2, b2, wqkv, bqkv, offs, out):
         w2_sb = held.tile([P, P], BF16, name="w2_sb")
         pe_sb = held.tile([P, AGENTS], BF16, name="pe_sb")
         wqkv_sb = held.tile([P, QKV_BLOCKS * P], BF16, name="wqkv_sb")
-        b2_sb = held.tile([P, 1], F32, name="b2_sb")
-        bqkv_sb = held.tile([P, QKV_BLOCKS], F32, name="bqkv_sb")
+        bias_rows = held.tile([QKV_BLOCKS + 1, P], F32, name="bias_rows")
+        bqkv_rows = bqkv.rearrange("(c p) o -> c (p o)", p=P)
         nc.sync.dma_start(hid_sb[:], hid)
         nc.scalar.dma_start(w2_sb[:], w2)
-        nc.scalar.dma_start(b2_sb[:], b2)
-        nc.sync.dma_start(wqkv_sb[:], wqkv)
-        nc.scalar.dma_start(pe_sb[:], pe)
+        nc.sync.dma_start(bias_rows[0:2, :], bqkv_rows[0:2, :])
+        nc.scalar.dma_start(bias_rows[2:3, :], bqkv_rows[2:3, :])
+        nc.scalar.dma_start(bias_rows[3:4, :], b2.rearrange("p o -> o p"))
         nc.sync.dma_start(offsets[:], offs)
-        with nc.allow_non_contiguous_dma(reason="bias: one float32 to a partition for each block"):
-            nc.sync.dma_start(bqkv_sb[:], bqkv.rearrange("(c p) o -> p (c o)", p=P))
+        nc.scalar.dma_start(pe_sb[:], pe)
+        nc.sync.dma_start(wqkv_sb[:], wqkv)
 
         ones = held.tile([P, P], F32, name="ones")
         nc.vector.memset(ones[:], 1.0)
@@ -42,6 +42,14 @@ def tile_reltok_kernel(tc, pe, hid, w2, b2, wqkv, bqkv, offs, out):
         nc.tensor.matmul(row_index[:], column_index[0:1, :], ones[0:1, 0:1], start=True, stop=True)
         identity = held.tile([P, P], BF16, name="identity")
         nc.vector.tensor_scalar(identity[:], column_index[:], row_index[:, 0:1], None, IS_EQUAL)
+
+        B = QKV_BLOCKS + 1
+        small_identity = held.tile([B, B], F32, name="small_identity")
+        nc.vector.tensor_scalar(small_identity[:], column_index[0:B, 0:B], row_index[0:B, 0:1], None, IS_EQUAL)
+        bias_ps = banks.tile([P, B], F32, name="bias_ps")
+        nc.tensor.matmul(bias_ps[:], bias_rows[:], small_identity[:], start=True, stop=True)
+        bias_sb = held.tile([P, B], F32, name="bias_sb")
+        nc.vector.tensor_copy(bias_sb[:], bias_ps[:])
 
         warmed = held.tile([P, 1], F32, name="warmed")
         nc.scalar.activation(warmed[:], ones[:, 0:1], IDENTITY)
@@ -56,7 +64,7 @@ def tile_reltok_kernel(tc, pe, hid, w2, b2, wqkv, bqkv, offs, out):
         nc.tensor.matmul(xin_bank[:], w2_sb[:], relu_hid[:], start=True, stop=True)
         nc.tensor.matmul(x_bank[:], w2_sb[:], relu_hid[:], start=True, stop=False)
         xin_bf = held.tile([P, TOKENS], BF16, name="xin_bf")
-        nc.vector.tensor_scalar(xin_bf[:], xin_bank[:], b2_sb[:, 0:1], None, ADD)
+        nc.vector.tensor_scalar(xin_bf[:], xin_bank[:], bias_sb[:, QKV_BLOCKS : QKV_BLOCKS + 1], None, ADD)
 
         looked_up = pe_sb[:].indirect(offsets[:])
         nc.tensor.matmul(x_bank[:], identity[:], looked_up, start=False, stop=True)
@@ -64,15 +72,15 @@ def tile_reltok_kernel(tc, pe, hid, w2, b2, wqkv, bqkv, offs, out):
             nc.tensor.matmul(qkv_banks[c][:], wqkv_sb[:, c * P : (c + 1) * P], looked_up, start=True, stop=False)
 
         x_sb = held.tile([P, TOKENS], F32, name="x_sb")
-        nc.scalar.activation(x_sb[:], x_bank[:], IDENTITY, bias=b2_sb[:, 0:1])
+        nc.scalar.activation(x_sb[:], x_bank[:], IDENTITY, bias=bias_sb[:, QKV_BLOCKS : QKV_BLOCKS + 1])
         nc.scalar.dma_start(out[QKV_BLOCKS * P : (QKV_BLOCKS + 1) * P, :], x_sb[:])
 
         for c in range(QKV_BLOCKS):
             nc.tensor.matmul(qkv_banks[c][:], wqkv_sb[:, c * P : (c + 1) * P], xin_bf[:], start=False, stop=True)
             block_sb = held.tile([P, TOKENS], F32, name=f"block_sb{c}")
             if c % 2 == 0:
-                nc.vector.tensor_scalar(block_sb[:], qkv_banks[c][:], bqkv_sb[:, c : c + 1], None, ADD)
+                nc.vector.tensor_scalar(block_sb[:], qkv_banks[c][:], bias_sb[:, c : c + 1], None, ADD)
                 nc.sync.dma_start(out[c * P : (c + 1) * P, :], block_sb[:])
             else:
-                nc.scalar.activation(block_sb[:], qkv_banks[c][:], IDENTITY, bias=bqkv_sb[:, c : c + 1])
+                nc.scalar.activation(block_sb[:], qkv_banks[c][:], IDENTITY, bias=bias_sb[:, c : c + 1])
                 nc.scalar.dma_start(out[c * P : (c + 1) * P, :], block_sb[:])

@@ -23,16 +23,16 @@ def tile_reltok_kernel(tc, pe, hid, w2, b2, wqkv, bqkv, offs, out):
         w2_sb = held.tile([P, P], BF16, name="w2_sb")
         pe_sb = held.tile([P, AGENTS], BF16, name="pe_sb")
         wqkv_sb = held.tile([P, QKV_BLOCKS * P], BF16, name="wqkv_sb")
-        bias_rows = held.tile([QKV_BLOCKS + 1, P], F32, name="bias_rows")
-        bqkv_rows = bqkv.rearrange("(c p) o -> c (p o)", p=P)
+        b2_sb = held.tile([P, 1], F32, name="b2_sb")
+        bqkv_sb = held.tile([P, QKV_BLOCKS], F32, name="bqkv_sb")
         nc.sync.dma_start(hid_sb[:], hid)
         nc.scalar.dma_start(w2_sb[:], w2)
-        nc.sync.dma_start(bias_rows[0:2, :], bqkv_rows[0:2, :])
-        nc.scalar.dma_start(bias_rows[2:3, :], bqkv_rows[2:3, :])
-        nc.scalar.dma_start(bias_rows[3:4, :], b2.rearrange("p o -> o p"))
         nc.sync.dma_start(offsets[:], offs)
         nc.scalar.dma_start(pe_sb[:], pe)
         nc.sync.dma_start(wqkv_sb[:], wqkv)
+        nc.scalar.dma_start(b2_sb[:], b2)
+        with nc.allow_non_contiguous_dma(reason="bias: one float32 to a partition for each block"):
+            nc.sync.dma_start(bqkv_sb[:], bqkv.rearrange("(c p) o -> p (c o)", p=P))
 
         ones = held.tile([P, P], F32, name="ones")
         nc.vector.memset(ones[:], 1.0)
@@ -42,14 +42,6 @@ def tile_reltok_kernel(tc, pe, hid, w2, b2, wqkv, bqkv, offs, out):
         nc.tensor.matmul(row_index[:], column_index[0:1, :], ones[0:1, 0:1], start=True, stop=True)
         identity = held.tile([P, P], BF16, name="identity")
         nc.vector.tensor_scalar(identity[:], column_index[:], row_index[:, 0:1], None, IS_EQUAL)
-
-        B = QKV_BLOCKS + 1
-        small_identity = held.tile([B, B], F32, name="small_identity")
-        nc.vector.tensor_scalar(small_identity[:], column_index[0:B, 0:B], row_index[0:B, 0:1], None, IS_EQUAL)
-        bias_ps = banks.tile([P, B], F32, name="bias_ps")
-        nc.tensor.matmul(bias_ps[:], bias_rows[:], small_identity[:], start=True, stop=True)
-        bias_sb = held.tile([P, B], F32, name="bias_sb")
-        nc.vector.tensor_copy(bias_sb[:], bias_ps[:])
 
         warmed = held.tile([P, 1], F32, name="warmed")
         nc.scalar.activation(warmed[:], ones[:, 0:1], IDENTITY)
@@ -64,7 +56,7 @@ def tile_reltok_kernel(tc, pe, hid, w2, b2, wqkv, bqkv, offs, out):
         nc.tensor.matmul(xin_bank[:], w2_sb[:], relu_hid[:], start=True, stop=True)
         nc.tensor.matmul(x_bank[:], w2_sb[:], relu_hid[:], start=True, stop=False)
         xin_bf = held.tile([P, TOKENS], BF16, name="xin_bf")
-        nc.vector.tensor_scalar(xin_bf[:], xin_bank[:], bias_sb[:, QKV_BLOCKS : QKV_BLOCKS + 1], None, ADD)
+        nc.vector.tensor_scalar(xin_bf[:], xin_bank[:], b2_sb[:, 0:1], None, ADD)
 
         looked_up = pe_sb[:].indirect(offsets[:])
         nc.tensor.matmul(x_bank[:], identity[:], looked_up, start=False, stop=True)
@@ -72,15 +64,15 @@ def tile_reltok_kernel(tc, pe, hid, w2, b2, wqkv, bqkv, offs, out):
             nc.tensor.matmul(qkv_banks[c][:], wqkv_sb[:, c * P : (c + 1) * P], looked_up, start=True, stop=False)
 
         x_sb = held.tile([P, TOKENS], F32, name="x_sb")
-        nc.scalar.activation(x_sb[:], x_bank[:], IDENTITY, bias=bias_sb[:, QKV_BLOCKS : QKV_BLOCKS + 1])
+        nc.scalar.activation(x_sb[:], x_bank[:], IDENTITY, bias=b2_sb[:, 0:1])
         nc.scalar.dma_start(out[QKV_BLOCKS * P : (QKV_BLOCKS + 1) * P, :], x_sb[:])
 
         for c in range(QKV_BLOCKS):
             nc.tensor.matmul(qkv_banks[c][:], wqkv_sb[:, c * P : (c + 1) * P], xin_bf[:], start=False, stop=True)
             block_sb = held.tile([P, TOKENS], F32, name=f"block_sb{c}")
             if c % 2 == 0:
-                nc.vector.tensor_scalar(block_sb[:], qkv_banks[c][:], bias_sb[:, c : c + 1], None, ADD)
+                nc.vector.tensor_scalar(block_sb[:], qkv_banks[c][:], bqkv_sb[:, c : c + 1], None, ADD)
                 nc.sync.dma_start(out[c * P : (c + 1) * P, :], block_sb[:])
             else:
-                nc.scalar.activation(block_sb[:], qkv_banks[c][:], IDENTITY, bias=bias_sb[:, c : c + 1])
+                nc.scalar.activation(block_sb[:], qkv_banks[c][:], IDENTITY, bias=bqkv_sb[:, c : c + 1])
                 nc.scalar.dma_start(out[c * P : (c + 1) * P, :], block_sb[:])

@@ -50,21 +50,22 @@ def tile_reltok_kernel(tc, pe, hid, w2, b2, wqkv, bqkv, offs, out):
         nc.vector.tensor_scalar_max(relu_hid[:], hid_sb[:], 0.0)
 
         xin_bank = banks.tile([P, TOKENS], F32, name="xin_bank")
-        x_bank = banks.tile([P, TOKENS], F32, name="x_bank")
+        picked_bank = banks.tile([P, TOKENS], F32, name="picked_bank")
         qkv_banks = [banks.tile([P, TOKENS], F32, name=f"qkv_bank{c}") for c in range(QKV_BLOCKS)]
 
         nc.tensor.matmul(xin_bank[:], w2_sb[:], relu_hid[:], start=True, stop=True)
-        nc.tensor.matmul(x_bank[:], w2_sb[:], relu_hid[:], start=True, stop=False)
         xin_bf = held.tile([P, TOKENS], BF16, name="xin_bf")
         nc.vector.tensor_scalar(xin_bf[:], xin_bank[:], b2_sb[:, 0:1], None, ADD)
 
         looked_up = pe_sb[:].indirect(offsets[:])
-        nc.tensor.matmul(x_bank[:], identity[:], looked_up, start=False, stop=True)
+        nc.tensor.matmul(picked_bank[:], identity[:], looked_up, start=True, stop=True)
         for c in range(QKV_BLOCKS):
             nc.tensor.matmul(qkv_banks[c][:], wqkv_sb[:, c * P : (c + 1) * P], looked_up, start=True, stop=False)
 
+        picked_sb = held.tile([P, TOKENS], F32, name="picked_sb")
+        nc.scalar.activation(picked_sb[:], picked_bank[:], IDENTITY, bias=b2_sb[:, 0:1])
         x_sb = held.tile([P, TOKENS], F32, name="x_sb")
-        nc.scalar.activation(x_sb[:], x_bank[:], IDENTITY, bias=b2_sb[:, 0:1])
+        nc.vector.tensor_tensor(x_sb[:], xin_bank[:], picked_sb[:], ADD)
         nc.scalar.dma_start(out[QKV_BLOCKS * P : (QKV_BLOCKS + 1) * P, :], x_sb[:])
 
         for c in range(QKV_BLOCKS):

@@ -8,6 +8,7 @@ P = 128
 AGENTS = 256
 TOKENS = 128
 QKV_BLOCKS = 3
+BLOCK = 32
 
 FLOPS = 2 * P * TOKENS * (P + QKV_BLOCKS * P)
 
@@ -23,16 +24,22 @@ def tile_reltok_kernel(tc, pe, hid, w2, b2, wqkv, bqkv, offs, out):
         w2_sb = held.tile([P, P], BF16, name="w2_sb")
         pe_sb = held.tile([P, AGENTS], BF16, name="pe_sb")
         wqkv_sb = held.tile([P, QKV_BLOCKS * P], BF16, name="wqkv_sb")
-        b2_sb = held.tile([P, 1], F32, name="b2_sb")
-        bqkv_sb = held.tile([P, QKV_BLOCKS], F32, name="bqkv_sb")
+        bias_rows = held.tile([P, (QKV_BLOCKS + 1) * BLOCK], F32, name="bias_rows", align_bytes=64)
+        bias_cols = held.tile([P, (QKV_BLOCKS + 1) * BLOCK], F32, name="bias_cols", align_bytes=64)
+        nc.gpsimd.memset(bias_rows[:], 0.0)
         nc.sync.dma_start(hid_sb[:], hid)
         nc.scalar.dma_start(w2_sb[:], w2)
         nc.sync.dma_start(offsets[:], offs)
         nc.scalar.dma_start(pe_sb[:], pe)
         nc.sync.dma_start(wqkv_sb[:], wqkv)
-        nc.scalar.dma_start(b2_sb[:], b2)
-        with nc.allow_non_contiguous_dma(reason="bias: one float32 to a partition for each block"):
-            nc.sync.dma_start(bqkv_sb[:], bqkv.rearrange("(c p) o -> p (c o)", p=P))
+        nc.scalar.dma_start(
+            bias_rows[0:P:BLOCK, QKV_BLOCKS * BLOCK : (QKV_BLOCKS + 1) * BLOCK],
+            b2.rearrange("(q r) o -> q (r o)", r=BLOCK),
+        )
+        nc.sync.dma_start(
+            bias_rows[0:P:BLOCK, 0 : QKV_BLOCKS * BLOCK].rearrange("q (c r) -> q c r", r=BLOCK),
+            bqkv.rearrange("(c q r) o -> q c (r o)", c=QKV_BLOCKS, r=BLOCK),
+        )
 
         ones = held.tile([P, P], F32, name="ones")
         nc.vector.memset(ones[:], 1.0)
@@ -48,6 +55,8 @@ def tile_reltok_kernel(tc, pe, hid, w2, b2, wqkv, bqkv, offs, out):
 
         relu_hid = held.tile([P, TOKENS], BF16, name="relu_hid")
         nc.vector.tensor_scalar_max(relu_hid[:], hid_sb[:], 0.0)
+        nc.vector.transpose(bias_cols[:], bias_rows[:])
+        b2_sb = bias_cols[:, QKV_BLOCKS * BLOCK : QKV_BLOCKS * BLOCK + 1]
 
         xin_bank = banks.tile([P, TOKENS], F32, name="xin_bank")
         picked_bank = banks.tile([P, TOKENS], F32, name="picked_bank")
@@ -55,7 +64,7 @@ def tile_reltok_kernel(tc, pe, hid, w2, b2, wqkv, bqkv, offs, out):
 
         nc.tensor.matmul(xin_bank[:], w2_sb[:], relu_hid[:], start=True, stop=True)
         xin_bf = held.tile([P, TOKENS], BF16, name="xin_bf")
-        nc.vector.tensor_scalar(xin_bf[:], xin_bank[:], b2_sb[:, 0:1], None, ADD)
+        nc.vector.tensor_scalar(xin_bf[:], xin_bank[:], b2_sb, None, ADD)
 
         looked_up = pe_sb[:].indirect(offsets[:])
         nc.tensor.matmul(picked_bank[:], identity[:], looked_up, start=True, stop=True)
@@ -63,7 +72,7 @@ def tile_reltok_kernel(tc, pe, hid, w2, b2, wqkv, bqkv, offs, out):
             nc.tensor.matmul(qkv_banks[c][:], wqkv_sb[:, c * P : (c + 1) * P], looked_up, start=True, stop=False)
 
         picked_sb = held.tile([P, TOKENS], F32, name="picked_sb")
-        nc.scalar.activation(picked_sb[:], picked_bank[:], IDENTITY, bias=b2_sb[:, 0:1])
+        nc.scalar.activation(picked_sb[:], picked_bank[:], IDENTITY, bias=b2_sb)
         x_sb = held.tile([P, TOKENS], F32, name="x_sb")
         nc.vector.tensor_tensor(x_sb[:], xin_bank[:], picked_sb[:], ADD)
         nc.scalar.dma_start(out[QKV_BLOCKS * P : (QKV_BLOCKS + 1) * P, :], x_sb[:])
@@ -72,8 +81,8 @@ def tile_reltok_kernel(tc, pe, hid, w2, b2, wqkv, bqkv, offs, out):
             nc.tensor.matmul(qkv_banks[c][:], wqkv_sb[:, c * P : (c + 1) * P], xin_bf[:], start=False, stop=True)
             block_sb = held.tile([P, TOKENS], F32, name=f"block_sb{c}")
             if c % 2 == 0:
-                nc.vector.tensor_scalar(block_sb[:], qkv_banks[c][:], bqkv_sb[:, c : c + 1], None, ADD)
+                nc.vector.tensor_scalar(block_sb[:], qkv_banks[c][:], bias_cols[:, c * BLOCK : c * BLOCK + 1], None, ADD)
                 nc.sync.dma_start(out[c * P : (c + 1) * P, :], block_sb[:])
             else:
-                nc.scalar.activation(block_sb[:], qkv_banks[c][:], IDENTITY, bias=bqkv_sb[:, c : c + 1])
+                nc.scalar.activation(block_sb[:], qkv_banks[c][:], IDENTITY, bias=bias_cols[:, c * BLOCK : c * BLOCK + 1])
                 nc.scalar.dma_start(out[c * P : (c + 1) * P, :], block_sb[:])

@@ -59,22 +59,21 @@ def tile_reltok_kernel(tc, pe, hid, w2, b2, wqkv, bqkv, offs, out):
         b2_sb = bias_cols[:, QKV_BLOCKS * BLOCK : QKV_BLOCKS * BLOCK + 1]
 
         xin_bank = banks.tile([P, TOKENS], F32, name="xin_bank")
-        picked_bank = banks.tile([P, TOKENS], F32, name="picked_bank")
+        x_bank = banks.tile([P, TOKENS], F32, name="x_bank")
         qkv_banks = [banks.tile([P, TOKENS], F32, name=f"qkv_bank{c}") for c in range(QKV_BLOCKS)]
 
         nc.tensor.matmul(xin_bank[:], w2_sb[:], relu_hid[:], start=True, stop=True)
+        nc.tensor.matmul(x_bank[:], w2_sb[:], relu_hid[:], start=True, stop=False)
         xin_bf = held.tile([P, TOKENS], BF16, name="xin_bf")
         nc.vector.tensor_scalar(xin_bf[:], xin_bank[:], b2_sb, None, ADD)
 
         looked_up = pe_sb[:].indirect(offsets[:])
-        nc.tensor.matmul(picked_bank[:], identity[:], looked_up, start=True, stop=True)
+        nc.tensor.matmul(x_bank[:], identity[:], looked_up, start=False, stop=True)
         for c in range(QKV_BLOCKS):
             nc.tensor.matmul(qkv_banks[c][:], wqkv_sb[:, c * P : (c + 1) * P], looked_up, start=True, stop=False)
 
-        picked_sb = held.tile([P, TOKENS], F32, name="picked_sb")
-        nc.scalar.activation(picked_sb[:], picked_bank[:], IDENTITY, bias=b2_sb)
         x_sb = held.tile([P, TOKENS], F32, name="x_sb")
-        nc.vector.tensor_tensor(x_sb[:], xin_bank[:], picked_sb[:], ADD)
+        nc.scalar.activation(x_sb[:], x_bank[:], IDENTITY, bias=b2_sb)
         nc.scalar.dma_start(out[QKV_BLOCKS * P : (QKV_BLOCKS + 1) * P, :], x_sb[:])
 
         for c in range(QKV_BLOCKS):

import concourse.mybir as mybir

BF16, F32, U16 = mybir.dt.bfloat16, mybir.dt.float32, mybir.dt.uint16
ADD, MULT, IS_EQUAL = mybir.AluOpType.add, mybir.AluOpType.mult, mybir.AluOpType.is_equal
IDENTITY = mybir.ActivationFunctionType.Identity

P = 128
AGENTS = 256
TOKENS = 128
QKV_BLOCKS = 3
BLOCK = 32

FLOPS = 2 * P * TOKENS * (P + QKV_BLOCKS * P)


def tile_reltok_kernel(tc, pe, hid, w2, b2, wqkv, bqkv, offs, out):
    nc = tc.nc
    with (
        tc.tile_pool(name="held", bufs=1) as held,
        tc.psum_pool(name="banks", bufs=1) as banks,
    ):
        offsets = held.tile([P, TOKENS // 16], U16, name="offsets")
        hid_sb = held.tile([P, TOKENS], BF16, name="hid_sb")
        w2_sb = held.tile([P, P], BF16, name="w2_sb")
        pe_sb = held.tile([P, AGENTS], BF16, name="pe_sb")
        wqkv_sb = held.tile([P, QKV_BLOCKS * P], BF16, name="wqkv_sb")
        bias_rows = held.tile([P, (QKV_BLOCKS + 1) * BLOCK], F32, name="bias_rows", align_bytes=64)
        bias_cols = held.tile([P, (QKV_BLOCKS + 1) * BLOCK], F32, name="bias_cols", align_bytes=64)
        nc.gpsimd.memset(bias_rows[:], 0.0)
        nc.sync.dma_start(hid_sb[:], hid)
        nc.scalar.dma_start(w2_sb[:], w2)
        nc.sync.dma_start(offsets[:], offs)
        nc.scalar.dma_start(pe_sb[:], pe)
        nc.sync.dma_start(wqkv_sb[:], wqkv)
        nc.scalar.dma_start(
            bias_rows[0:P:BLOCK, QKV_BLOCKS * BLOCK : (QKV_BLOCKS + 1) * BLOCK],
            b2.rearrange("(q r) o -> q (r o)", r=BLOCK),
        )
        nc.sync.dma_start(
            bias_rows[0:P:BLOCK, 0 : QKV_BLOCKS * BLOCK].rearrange("q (c r) -> q c r", r=BLOCK),
            bqkv.rearrange("(c q r) o -> q c (r o)", c=QKV_BLOCKS, r=BLOCK),
        )

        ones = held.tile([P, P], F32, name="ones")
        nc.vector.memset(ones[:], 1.0)
        column_index = held.tile([P, P], F32, name="column_index")
        nc.vector.tensor_tensor_scan(column_index[:], ones[:], ones[:], -1.0, MULT, ADD)
        row_index = banks.tile([P, 1], F32, name="row_index")
        nc.tensor.matmul(row_index[:], column_index[0:1, :], ones[0:1, 0:1], start=True, stop=True)
        identity = held.tile([P, P], BF16, name="identity")
        nc.vector.tensor_scalar(identity[:], column_index[:], row_index[:, 0:1], None, IS_EQUAL)

        warmed = held.tile([P, 1], F32, name="warmed")
        nc.scalar.activation(warmed[:], ones[:, 0:1], IDENTITY)

        relu_hid = held.tile([P, TOKENS], BF16, name="relu_hid")
        nc.vector.tensor_scalar_max(relu_hid[:], hid_sb[:], 0.0)
        nc.vector.transpose(bias_cols[:], bias_rows[:])
        b2_sb = bias_cols[:, QKV_BLOCKS * BLOCK : QKV_BLOCKS * BLOCK + 1]

        xin_bank = banks.tile([P, TOKENS], F32, name="xin_bank")
        x_bank = banks.tile([P, TOKENS], F32, name="x_bank")
        qkv_banks = [banks.tile([P, TOKENS], F32, name=f"qkv_bank{c}") for c in range(QKV_BLOCKS)]

        nc.tensor.matmul(xin_bank[:], w2_sb[:], relu_hid[:], start=True, stop=True)
        nc.tensor.matmul(x_bank[:], w2_sb[:], relu_hid[:], start=True, stop=False)
        xin_bf = held.tile([P, TOKENS], BF16, name="xin_bf")
        nc.vector.tensor_scalar(xin_bf[:], xin_bank[:], b2_sb, None, ADD)

        looked_up = pe_sb[:].indirect(offsets[:])
        nc.tensor.matmul(x_bank[:], identity[:], looked_up, start=False, stop=True)
        for c in range(QKV_BLOCKS):
            nc.tensor.matmul(qkv_banks[c][:], wqkv_sb[:, c * P : (c + 1) * P], looked_up, start=True, stop=False)

        x_sb = held.tile([P, TOKENS], F32, name="x_sb")
        nc.scalar.activation(x_sb[:], x_bank[:], IDENTITY, bias=b2_sb)
        nc.scalar.dma_start(out[QKV_BLOCKS * P : (QKV_BLOCKS + 1) * P, :], x_sb[:])

        for c in range(QKV_BLOCKS):
            nc.tensor.matmul(qkv_banks[c][:], wqkv_sb[:, c * P : (c + 1) * P], xin_bf[:], start=False, stop=True)
            block_sb = held.tile([P, TOKENS], F32, name=f"block_sb{c}")
            if c % 2 == 0:
                nc.vector.tensor_scalar(block_sb[:], qkv_banks[c][:], bias_cols[:, c * BLOCK : c * BLOCK + 1], None, ADD)
                nc.sync.dma_start(out[c * P : (c + 1) * P, :], block_sb[:])
            else:
                nc.scalar.activation(block_sb[:], qkv_banks[c][:], IDENTITY, bias=bias_cols[:, c * BLOCK : c * BLOCK + 1])
                nc.scalar.dma_start(out[c * P : (c + 1) * P, :], block_sb[:])
